import numpy as np
import ml_dtypes


def mxq(x, axis, fmt="e4m3"):
    dtype, down = {"e4m3": (ml_dtypes.float8_e4m3fn, 7), "e5m2": (ml_dtypes.float8_e5m2, 14)}[fmt]
    v = np.moveaxis(np.asarray(x, np.float32).astype(ml_dtypes.bfloat16).astype(np.float64), axis, -1)
    blocks = v.reshape(v.shape[:-1] + (-1, 32))
    amax = np.abs(blocks).max(-1, keepdims=True)
    byte = np.maximum(np.where(amax > 0, np.frexp(amax)[1] - 1 + 127, 0) - down, 1)
    scale = np.exp2(byte - 127.0)
    codes = (blocks / scale).astype(np.float32).astype(dtype).astype(np.float64)
    return np.moveaxis((codes * scale).reshape(v.shape), -1, axis)


WIDE = False


def mx_kscale(k):
    if not WIDE:
        return np.ones(k)
    levels = np.array([10, -10, 5, -5, 0])
    a = np.random.permutation(np.resize(levels, k // 512 * 4)).reshape(k // 512, 4)
    idx = np.arange(k)
    return np.exp2(a[idx // 512, idx % 128 // 32])


BF16 = ml_dtypes.bfloat16


def bf(x):
    return np.asarray(x, np.float32).astype(BF16)


def f64(x):
    return np.asarray(x).astype(np.float64)


B, T, C, H, NOPE, ROPE, VD, LORA = 4, 1024, 1024, 2, 128, 512, 128, 512
EPS = 1e-6
HALF = ROPE // 2
KVW = H * (NOPE + VD)


def make_freq_cis():
    inv = 1.0 / (10000.0 ** (np.arange(0, ROPE, 2) / ROPE))
    ang = np.outer(np.arange(T), inv)
    return np.stack([np.cos(ang), np.sin(ang)], -1)


def apply_rope(v, fc):
    vr = v.reshape(B, T, HALF, 2)
    real = vr[..., 0] * fc[..., 0] - vr[..., 1] * fc[..., 1]
    imag = vr[..., 1] * fc[..., 0] + vr[..., 0] * fc[..., 1]
    return np.stack([real, imag], -1).reshape(B, T, ROPE)


def setup_inputs():
    s, t = mx_kscale(C), mx_kscale(LORA)
    return {"x": bf(np.random.standard_normal((B, T, C)) * s),
            "freq_cis": bf(make_freq_cis()),
            "Wckv": bf(np.random.standard_normal((C, LORA + ROPE)) / np.sqrt(C) / s[:, None]),
            "kv_norm_w": bf((1.0 + 0.1 * np.random.standard_normal(LORA)) * t),
            "Wdkv": bf(np.random.standard_normal((LORA, KVW)) / np.sqrt(LORA) / t[:, None])}


def reference(x, freq_cis, Wckv, kv_norm_w, Wdkv):
    ckv = mxq(f64(x), 2, "e4m3") @ mxq(f64(Wckv), 0, "e4m3")
    kv_lat, k_rope = ckv[..., :LORA], ckv[..., LORA:]
    k_rope = apply_rope(k_rope, f64(freq_cis))
    lat_n = kv_lat / np.sqrt(np.mean(kv_lat * kv_lat, -1, keepdims=True) + EPS) * f64(kv_norm_w)
    kv = mxq(lat_n, 2, "e4m3") @ mxq(f64(Wdkv), 0, "e4m3")
    return kv, k_rope

@@ -1,0 +1,284 @@
+from contextlib import ExitStack
+
+import concourse.mybir as mybir
+from concourse.masks import make_identity
+
+F32 = mybir.dt.float32
+BF16 = mybir.dt.bfloat16
+U32 = mybir.dt.uint32
+U8 = mybir.dt.uint8
+FP8X4 = mybir.dt.float8_e4m3fn_x4
+ALU = mybir.AluOpType
+ACT = mybir.ActivationFunctionType
+
+B, T, C, LORA, ROPE, KVW = 4, 1024, 1024, 512, 512, 512
+EPS = 1e-6
+P = 128
+PACK = 4
+K_PASS = P * PACK
+PASSES = C // K_PASS
+J = T // P
+TILES = B * J
+HALF = ROPE // 2
+X_TILES = 2
+OUT_TILES = 2
+
+FLOPS = 2 * B * T * C * (LORA + ROPE) + 2 * B * T * LORA * KVW
+
+
+def regroup(nc, grouped, raw, cols):
+    split = cols * 5 // 8
+    for copy, lo, hi in ((nc.vector.tensor_copy, 0, split), (nc.scalar.copy, split, cols)):
+        copy(
+            out=grouped[:, lo:hi, :].rearrange("p (c i) t -> p c t i", i=4),
+            in_=raw[:, :, lo:hi].rearrange("p t (c i) -> p c t i", i=4),
+        )
+
+
+def tile_multiheadlatentattention_pa_t_kernel(
+    tc, x, freq_cis, Wckv, kv_norm_w, Wdkv, out_0, out_1
+):
+    nc = tc.nc
+    x_view = x.rearrange("b (p j) c -> b p j c", j=J)
+    table_view = freq_cis.rearrange("(p j) i two -> p j (i two)", j=J)
+    kv_view = out_0.rearrange("b (p j) f -> b p j f", j=J)
+    rope_view = out_1.rearrange("b (p j) f -> b p j f", j=J)
+
+    with ExitStack() as ctx:
+        keep = ctx.enter_context(tc.tile_pool(name="keep", bufs=1))
+        x_pool = ctx.enter_context(tc.tile_pool(name="x_pool", bufs=TILES // X_TILES))
+        stage = ctx.enter_context(tc.tile_pool(name="stage", bufs=2))
+        work = ctx.enter_context(tc.tile_pool(name="work", bufs=3))
+        small = ctx.enter_context(tc.tile_pool(name="small", bufs=4))
+        outs = ctx.enter_context(tc.tile_pool(name="outs", bufs=3))
+        psum = ctx.enter_context(tc.psum_pool(name="psum", bufs=1))
+
+        eps = keep.tile([P, 1], F32)
+        nc.vector.memset(eps[:], EPS)
+        warm = keep.tile([P, 1], F32)
+        nc.scalar.activation(out=warm[:], in_=eps[:], func=ACT.Sqrt)
+        ident_f32 = keep.tile([P, P], F32)
+        make_identity(nc, ident_f32[:])
+        ident_bf16 = keep.tile([P, P], BF16)
+        make_identity(nc, ident_bf16[:])
+        ones = keep.tile([P, P], BF16)
+        nc.vector.memset(ones[:], 1.0)
+        gain_rows = keep.tile([P, LORA], BF16)
+        nc.vector.memset(gain_rows[:], 0.0)
+
+        x_chunks = []
+
+        def load_x(chunk):
+            b, j0 = divmod(chunk * X_TILES, J)
+            x_sb = x_pool.tile([P, X_TILES, C], BF16, name="x_sb")
+            nc.sync.dma_start(out=x_sb[:], in_=x_view[b, :, j0 : j0 + X_TILES, :])
+            x_chunks.append(x_sb)
+
+        load_x(0)
+        w_raws = []
+        for g in range(PASSES):
+            w_raw = stage.tile([P, PACK, LORA + ROPE], BF16, name="w_raw")
+            for u in range(2):
+                k0 = K_PASS * g + 2 * P * u
+                nc.sync.dma_start(
+                    out=w_raw[:, 2 * u : 2 * u + 2, :],
+                    in_=Wckv[k0 : k0 + 2 * P, :].rearrange("(q e) c -> q e c", e=2),
+                )
+            w_raws.append(w_raw)
+        nc.sync.dma_start(out=gain_rows[0:1, :], in_=kv_norm_w.unsqueeze(0))
+        table = keep.tile([P, J, ROPE], BF16)
+        nc.sync.dma_start(out=table[:, 0 : J // 2, :], in_=table_view[:, 0 : J // 2, :])
+        wd_raw = stage.tile([P, PACK, KVW], BF16, name="wd_raw", bufs=1)
+        nc.sync.dma_start(out=wd_raw[:], in_=Wdkv.rearrange("(t p) n -> p t n", p=P))
+        load_x(1)
+        nc.sync.dma_start(out=table[:, J // 2 : J, :], in_=table_view[:, J // 2 : J, :])
+        for chunk in range(2, TILES // X_TILES):
+            load_x(chunk)
+
+        w_codes = keep.tile([P, PASSES, LORA + ROPE], U32, align_bytes=64)
+        w_scales = keep.tile([P, PASSES, LORA + ROPE], U8, align_bytes=64)
+        for g in range(PASSES):
+            for n0 in (0, LORA):
+                w_grouped = stage.tile([P, LORA, PACK], BF16, name="w_grouped", bufs=4, align_bytes=64)
+                regroup(nc, w_grouped, w_raws[g][:, :, n0 : n0 + LORA], LORA)
+                nc.vector.quantize_mx(
+                    out=w_codes[:, g, n0 : n0 + LORA].bitcast(FP8X4),
+                    scales=w_scales[:, g, n0 : n0 + LORA],
+                    in_=w_grouped[:].rearrange("p c t -> p (c t)"),
+                )
+        wd_codes = keep.tile([P, KVW], U32, align_bytes=64)
+        wd_scales = keep.tile([P, KVW], U8, align_bytes=64)
+        wd_grouped = stage.tile([P, KVW, PACK], BF16, name="w_grouped", bufs=4, align_bytes=64)
+        regroup(nc, wd_grouped, wd_raw, KVW)
+        nc.vector.quantize_mx(
+            out=wd_codes[:].bitcast(FP8X4),
+            scales=wd_scales[:],
+            in_=wd_grouped[:].rearrange("p c t -> p (c t)"),
+        )
+
+        gain_ps = psum.tile([P, LORA], F32, tag="kv")
+        nc.tensor.matmul(gain_ps[:], lhsT=ones[:], rhs=gain_rows[:], start=True, stop=True)
+        gain = keep.tile([P, LORA], F32)
+        nc.scalar.copy(out=gain[:], in_=gain_ps[:])
+
+        live = {}
+
+        def transpose_x(i):
+            chunk, jj = divmod(i, X_TILES)
+            words = x_chunks[chunk][:, jj, :].bitcast(F32)
+            xt = psum.tile([P, PASSES, 2, P], F32, tag="xt", bufs=2)
+            for g in range(PASSES):
+                for u in range(2):
+                    w0 = (2 * g + u) * P
+                    nc.tensor.transpose(xt[:, g, u, :], words[:, w0 : w0 + P], ident_f32[:])
+            live["xt", i] = xt
+
+        def group_x(i):
+            xt = live["xt", i]
+            x_grouped = work.tile([P, PASSES * P * PACK], BF16, align_bytes=64)
+            nc.scalar.copy(
+                out=x_grouped[:].bitcast(F32).rearrange("p (g r u) -> p g r u", g=PASSES, u=2),
+                in_=xt[:].rearrange("p g u r -> p g r u"),
+            )
+            live["x_grouped", i] = x_grouped
+
+        def quantise_x(i):
+            x_grouped = live["x_grouped", i]
+            x_codes = work.tile([P, PASSES * P], U32, align_bytes=64)
+            x_scales = work.tile([P, PASSES * P], U8, align_bytes=64)
+            nc.vector.quantize_mx(out=x_codes[:].bitcast(FP8X4), scales=x_scales[:], in_=x_grouped[:])
+            live["x_mx", i] = (x_codes, x_scales)
+
+        def first_matmul(i):
+            x_codes, x_scales = live["x_mx", i]
+            lat = psum.tile([P, LORA], F32, tag="lat", bufs=2)
+            kr = psum.tile([P, ROPE], F32, tag="kr", bufs=2)
+            for acc, n0 in ((lat, 0), (kr, LORA)):
+                for g in range(PASSES):
+                    tokens = slice(g * P, (g + 1) * P)
+                    nc.tensor.matmul_mx(
+                        out=acc[:],
+                        lhsT=x_codes[:, tokens].bitcast(FP8X4),
+                        lhsT_scale=x_scales[:, tokens],
+                        rhs=w_codes[:, g, n0 : n0 + LORA].bitcast(FP8X4),
+                        rhs_scale=w_scales[:, g, n0 : n0 + LORA],
+                        start=(g == 0),
+                        stop=(g == PASSES - 1),
+                    )
+            live["lat", i] = lat
+            live["kr", i] = kr
+
+        def mean_square(i):
+            lat = live["lat", i]
+            squares = work.tile([P, LORA], BF16)
+            sum_sq = small.tile([P, 1], F32)
+            nc.scalar.activation(out=squares[:], in_=lat[:], func=ACT.Square, accum_out=sum_sq[:])
+            rms = small.tile([P, 1], F32)
+            nc.scalar.activation(out=rms[:], in_=sum_sq[:], func=ACT.Sqrt, bias=eps[:], scale=1.0 / LORA)
+            live["rms", i] = rms
+
+        def rotate_products(i):
+            kr = live["kr", i][:].rearrange("p (i e) -> p i e", e=2)
+            cos_sin = table[:, i % J, :].rearrange("p (i two) -> p i two", two=2)
+            by_cos = work.tile([P, HALF, 2], F32)
+            nc.vector.tensor_tensor(
+                out=by_cos[:], in0=kr, in1=cos_sin[:, :, 0:1].to_broadcast([P, HALF, 2]), op=ALU.mult
+            )
+            by_sin = work.tile([P, 2, HALF], F32)
+            nc.vector.scalar_tensor_tensor(
+                out=by_sin[:, 0, :], in0=kr[:, :, 1], scalar=-1.0, in1=cos_sin[:, :, 1],
+                op0=ALU.mult, op1=ALU.mult,
+            )
+            nc.vector.tensor_tensor(out=by_sin[:, 1, :], in0=kr[:, :, 0], in1=cos_sin[:, :, 1], op=ALU.mult)
+            live["products", i] = (by_cos, by_sin)
+
+        def normalise(i):
+            lat = live["lat", i]
+            rms = live["rms", i]
+            inv_rms = small.tile([P, 1], F32)
+            nc.vector.reciprocal(out=inv_rms[:], in_=rms[:])
+            n_bf16 = work.tile([P, LORA], BF16)
+            nc.vector.scalar_tensor_tensor(
+                out=n_bf16[:], in0=lat[:], scalar=inv_rms[:], in1=gain[:], op0=ALU.mult, op1=ALU.mult
+            )
+            live["n", i] = n_bf16
+
+        def out_slot(name, i):
+            if i % OUT_TILES == 0:
+                live[name] = outs.tile([P, OUT_TILES, KVW], F32, name=name)
+            return live[name]
+
+        def store(name, view, i):
+            if i % OUT_TILES == OUT_TILES - 1:
+                b, j = divmod(i, J)
+                nc.sync.dma_start(out=view[b, :, j + 1 - OUT_TILES : j + 1, :], in_=live[name][:])
+
+        def rotate_sum(i):
+            by_cos, by_sin = live["products", i]
+            rope_sb = out_slot("rope_sb", i)
+            nc.gpsimd.tensor_tensor(
+                out=rope_sb[:, i % OUT_TILES, :].rearrange("p (i e) -> p i e", e=2),
+                in0=by_cos[:],
+                in1=by_sin[:].rearrange("p e i -> p i e"),
+                op=ALU.add,
+            )
+            store("rope_sb", rope_view, i)
+
+        def transpose_n(i):
+            n_bf16 = live["n", i]
+            nt = psum.tile([P, PACK, P], BF16, tag="nt")
+            for t in range(PACK):
+                nc.tensor.transpose(nt[:, t, :], n_bf16[:, t * P : (t + 1) * P], ident_bf16[:])
+            live["nt", i] = nt
+
+        def group_n(i):
+            nt = live["nt", i]
+            n_grouped = work.tile([P, P, PACK], BF16, align_bytes=64)
+            nc.scalar.copy(out=n_grouped[:], in_=nt[:].rearrange("p t r -> p r t"))
+            live["n_grouped", i] = n_grouped
+
+        def quantise_n(i):
+            n_grouped = live["n_grouped", i]
+            n_codes = work.tile([P, P], U32, align_bytes=64)
+            n_scales = work.tile([P, P], U8, align_bytes=64)
+            nc.vector.quantize_mx(
+                out=n_codes[:].bitcast(FP8X4), scales=n_scales[:],
+                in_=n_grouped[:].rearrange("p r t -> p (r t)"),
+            )
+            live["n_mx", i] = (n_codes, n_scales)
+
+        def second_matmul(i):
+            n_codes, n_scales = live["n_mx", i]
+            kv = psum.tile([P, KVW], F32, tag="kv")
+            nc.tensor.matmul_mx(
+                out=kv[:],
+                lhsT=n_codes[:].bitcast(FP8X4), lhsT_scale=n_scales[:],
+                rhs=wd_codes[:].bitcast(FP8X4), rhs_scale=wd_scales[:],
+                start=True, stop=True,
+            )
+            live["kv", i] = kv
+
+        def copy_kv(i):
+            kv = live["kv", i]
+            kv_sb = out_slot("kv_sb", i)
+            nc.scalar.copy(out=kv_sb[:, i % OUT_TILES, :], in_=kv[:])
+            store("kv_sb", kv_view, i)
+
+        def run(stage_fn, i):
+            if 0 <= i < TILES:
+                stage_fn(i)
+
+        for s in range(TILES + 4):
+            run(transpose_x, s)
+            run(transpose_n, s - 3)
+            run(group_x, s)
+            run(group_n, s - 3)
+            run(first_matmul, s - 1)
+            run(second_matmul, s - 4)
+            run(mean_square, s - 1)
+            run(copy_kv, s - 4)
+            run(rotate_products, s - 2)
+            run(quantise_x, s)
+            run(normalise, s - 2)
+            run(rotate_sum, s - 2)
+            run(quantise_n, s - 3)

@@ -22,6 +22,7 @@ TILES = B * J
 HALF = ROPE // 2
 X_TILES = 2
 OUT_TILES = 2
+X_LEAD = 2
 
 FLOPS = 2 * B * T * C * (LORA + ROPE) + 2 * B * T * LORA * KVW
 
@@ -52,6 +53,7 @@ def tile_multiheadlatentattention_pa_t_kernel(
         small = ctx.enter_context(tc.tile_pool(name="small", bufs=4))
         outs = ctx.enter_context(tc.tile_pool(name="outs", bufs=3))
         psum = ctx.enter_context(tc.psum_pool(name="psum", bufs=1))
+        ctx.enter_context(tc.manual_schedule())
 
         eps = keep.tile([P, 1], F32)
         nc.vector.memset(eps[:], EPS)
@@ -75,6 +77,7 @@ def tile_multiheadlatentattention_pa_t_kernel(
             x_chunks.append(x_sb)
 
         load_x(0)
+        nc.sync.dma_start(out=gain_rows[0:1, :], in_=kv_norm_w.unsqueeze(0))
         w_raws = []
         for g in range(PASSES):
             w_raw = stage.tile([P, PACK, LORA + ROPE], BF16, name="w_raw")
@@ -85,7 +88,6 @@ def tile_multiheadlatentattention_pa_t_kernel(
                     in_=Wckv[k0 : k0 + 2 * P, :].rearrange("(q e) c -> q e c", e=2),
                 )
             w_raws.append(w_raw)
-        nc.sync.dma_start(out=gain_rows[0:1, :], in_=kv_norm_w.unsqueeze(0))
         table = keep.tile([P, J, ROPE], BF16)
         nc.sync.dma_start(out=table[:, 0 : J // 2, :], in_=table_view[:, 0 : J // 2, :])
         wd_raw = stage.tile([P, PACK, KVW], BF16, name="wd_raw", bufs=1)
@@ -97,29 +99,9 @@ def tile_multiheadlatentattention_pa_t_kernel(
 
         w_codes = keep.tile([P, PASSES, LORA + ROPE], U32, align_bytes=64)
         w_scales = keep.tile([P, PASSES, LORA + ROPE], U8, align_bytes=64)
-        for g in range(PASSES):
-            for n0 in (0, LORA):
-                w_grouped = stage.tile([P, LORA, PACK], BF16, name="w_grouped", bufs=4, align_bytes=64)
-                regroup(nc, w_grouped, w_raws[g][:, :, n0 : n0 + LORA], LORA)
-                nc.vector.quantize_mx(
-                    out=w_codes[:, g, n0 : n0 + LORA].bitcast(FP8X4),
-                    scales=w_scales[:, g, n0 : n0 + LORA],
-                    in_=w_grouped[:].rearrange("p c t -> p (c t)"),
-                )
         wd_codes = keep.tile([P, KVW], U32, align_bytes=64)
         wd_scales = keep.tile([P, KVW], U8, align_bytes=64)
-        wd_grouped = stage.tile([P, KVW, PACK], BF16, name="w_grouped", bufs=4, align_bytes=64)
-        regroup(nc, wd_grouped, wd_raw, KVW)
-        nc.vector.quantize_mx(
-            out=wd_codes[:].bitcast(FP8X4),
-            scales=wd_scales[:],
-            in_=wd_grouped[:].rearrange("p c t -> p (c t)"),
-        )
-
-        gain_ps = psum.tile([P, LORA], F32, tag="kv")
-        nc.tensor.matmul(gain_ps[:], lhsT=ones[:], rhs=gain_rows[:], start=True, stop=True)
         gain = keep.tile([P, LORA], F32)
-        nc.scalar.copy(out=gain[:], in_=gain_ps[:])
 
         live = {}
 
@@ -144,8 +126,8 @@ def tile_multiheadlatentattention_pa_t_kernel(
 
         def quantise_x(i):
             x_grouped = live["x_grouped", i]
-            x_codes = work.tile([P, PASSES * P], U32, align_bytes=64)
-            x_scales = work.tile([P, PASSES * P], U8, align_bytes=64)
+            x_codes = work.tile([P, PASSES * P], U32, bufs=X_LEAD + 2, align_bytes=64)
+            x_scales = work.tile([P, PASSES * P], U8, bufs=X_LEAD + 2, align_bytes=64)
             nc.vector.quantize_mx(out=x_codes[:].bitcast(FP8X4), scales=x_scales[:], in_=x_grouped[:])
             live["x_mx", i] = (x_codes, x_scales)
 
@@ -264,21 +246,49 @@ def tile_multiheadlatentattention_pa_t_kernel(
             nc.scalar.copy(out=kv_sb[:, i % OUT_TILES, :], in_=kv[:])
             store("kv_sb", kv_view, i)
 
+        for i in range(X_LEAD):
+            transpose_x(i)
+            group_x(i)
+            quantise_x(i)
+
+        w_pieces = [
+            (w_raws[g][:, :, n0 : n0 + LORA], w_codes[:, g, n0 : n0 + LORA], w_scales[:, g, n0 : n0 + LORA])
+            for g in range(PASSES)
+            for n0 in (0, LORA)
+        ]
+        w_pieces.append((wd_raw[:], wd_codes[:], wd_scales[:]))
+        grouped_pieces = []
+        for k in range(len(w_pieces) + 1):
+            if k < len(w_pieces):
+                w_grouped = stage.tile([P, LORA, PACK], BF16, bufs=4, align_bytes=64)
+                regroup(nc, w_grouped, w_pieces[k][0], LORA)
+                grouped_pieces.append(w_grouped)
+            if k > 0:
+                nc.vector.quantize_mx(
+                    out=w_pieces[k - 1][1].bitcast(FP8X4),
+                    scales=w_pieces[k - 1][2],
+                    in_=grouped_pieces[k - 1][:].rearrange("p c t -> p (c t)"),
+                )
+
+        gain_ps = psum.tile([P, LORA], F32, tag="kv")
+        nc.tensor.matmul(gain_ps[:], lhsT=ones[:], rhs=gain_rows[:], start=True, stop=True)
+        nc.scalar.copy(out=gain[:], in_=gain_ps[:])
+
         def run(stage_fn, i):
             if 0 <= i < TILES:
                 stage_fn(i)
 
-        for s in range(TILES + 4):
-            run(transpose_x, s)
-            run(transpose_n, s - 3)
-            run(group_x, s)
-            run(group_n, s - 3)
-            run(first_matmul, s - 1)
-            run(second_matmul, s - 4)
-            run(mean_square, s - 1)
-            run(copy_kv, s - 4)
-            run(rotate_products, s - 2)
-            run(quantise_x, s)
-            run(normalise, s - 2)
-            run(rotate_sum, s - 2)
-            run(quantise_n, s - 3)
+        for s in range(TILES + 3):
+            run(transpose_x, s + X_LEAD)
+            run(transpose_n, s - 2)
+            run(group_x, s + X_LEAD)
+            run(group_n, s - 2)
+            run(first_matmul, s)
+            run(second_matmul, s - 3)
+            run(mean_square, s)
+            run(copy_kv, s - 3)
+            run(normalise, s - 1)
+            run(rotate_products, s - 1)
+            run(quantise_x, s + X_LEAD)
+            run(quantise_n, s - 2)
+            run(rotate_sum, s - 1)

@@ -17,12 +17,13 @@ P = 128
 PACK = 4
 K_PASS = P * PACK
 PASSES = C // K_PASS
+assert PASSES == 2
 J = T // P
 TILES = B * J
 HALF = ROPE // 2
-X_TILES = 2
 OUT_TILES = 2
 X_LEAD = 2
+ROPE_LAG = 2
 
 FLOPS = 2 * B * T * C * (LORA + ROPE) + 2 * B * T * LORA * KVW
 
@@ -47,7 +48,7 @@ def tile_multiheadlatentattention_pa_t_kernel(
 
     with ExitStack() as ctx:
         keep = ctx.enter_context(tc.tile_pool(name="keep", bufs=1))
-        x_pool = ctx.enter_context(tc.tile_pool(name="x_pool", bufs=TILES // X_TILES))
+        x_pool = ctx.enter_context(tc.tile_pool(name="x_pool", bufs=TILES))
         stage = ctx.enter_context(tc.tile_pool(name="stage", bufs=2))
         work = ctx.enter_context(tc.tile_pool(name="work", bufs=3))
         small = ctx.enter_context(tc.tile_pool(name="small", bufs=4))
@@ -68,34 +69,41 @@ def tile_multiheadlatentattention_pa_t_kernel(
         gain_rows = keep.tile([P, LORA], BF16)
         nc.vector.memset(gain_rows[:], 0.0)
 
-        x_chunks = []
+        x_tiles = []
 
-        def load_x(chunk):
-            b, j0 = divmod(chunk * X_TILES, J)
-            x_sb = x_pool.tile([P, X_TILES, C], BF16, name="x_sb")
-            nc.sync.dma_start(out=x_sb[:], in_=x_view[b, :, j0 : j0 + X_TILES, :])
-            x_chunks.append(x_sb)
+        def load_x(count):
+            for i in range(len(x_tiles), len(x_tiles) + count):
+                b, j = divmod(i, J)
+                x_sb = x_pool.tile([P, C], BF16, name="x_sb")
+                nc.sync.dma_start(out=x_sb[:], in_=x_view[b, :, j, :])
+                x_tiles.append(x_sb)
 
-        load_x(0)
-        nc.sync.dma_start(out=gain_rows[0:1, :], in_=kv_norm_w.unsqueeze(0))
-        w_raws = []
-        for g in range(PASSES):
-            w_raw = stage.tile([P, PACK, LORA + ROPE], BF16, name="w_raw")
-            for u in range(2):
-                k0 = K_PASS * g + 2 * P * u
-                nc.sync.dma_start(
-                    out=w_raw[:, 2 * u : 2 * u + 2, :],
-                    in_=Wckv[k0 : k0 + 2 * P, :].rearrange("(q e) c -> q e c", e=2),
-                )
-            w_raws.append(w_raw)
+        def load_w_half(n0):
+            raws = []
+            for g in range(PASSES):
+                w_raw = stage.tile([P, PACK, LORA], BF16, name="w_raw", bufs=2 * PASSES + 1)
+                for u in range(2):
+                    k0 = K_PASS * g + 2 * P * u
+                    nc.sync.dma_start(
+                        out=w_raw[:, 2 * u : 2 * u + 2, :],
+                        in_=Wckv[k0 : k0 + 2 * P, n0 : n0 + LORA].rearrange("(q e) c -> q e c", e=2),
+                    )
+                raws.append(w_raw)
+            return raws
+
         table = keep.tile([P, J, ROPE], BF16)
-        nc.sync.dma_start(out=table[:, 0 : J // 2, :], in_=table_view[:, 0 : J // 2, :])
-        wd_raw = stage.tile([P, PACK, KVW], BF16, name="wd_raw", bufs=1)
-        nc.sync.dma_start(out=wd_raw[:], in_=Wdkv.rearrange("(t p) n -> p t n", p=P))
         load_x(1)
+        lat_raws = load_w_half(0)
+        nc.sync.dma_start(out=gain_rows[0:1, :], in_=kv_norm_w.unsqueeze(0))
+        load_x(2)
+        rope_raws = load_w_half(LORA)
+        load_x(1)
+        nc.sync.dma_start(out=table[:, 0 : J // 2, :], in_=table_view[:, 0 : J // 2, :])
+        wd_raw = stage.tile([P, PACK, KVW], BF16, name="w_raw", bufs=2 * PASSES + 1)
+        nc.sync.dma_start(out=wd_raw[:], in_=Wdkv.rearrange("(t p) n -> p t n", p=P))
+        load_x(2)
         nc.sync.dma_start(out=table[:, J // 2 : J, :], in_=table_view[:, J // 2 : J, :])
-        for chunk in range(2, TILES // X_TILES):
-            load_x(chunk)
+        load_x(TILES - len(x_tiles))
 
         w_codes = keep.tile([P, PASSES, LORA + ROPE], U32, align_bytes=64)
         w_scales = keep.tile([P, PASSES, LORA + ROPE], U8, align_bytes=64)
@@ -106,8 +114,7 @@ def tile_multiheadlatentattention_pa_t_kernel(
         live = {}
 
         def transpose_x(i):
-            chunk, jj = divmod(i, X_TILES)
-            words = x_chunks[chunk][:, jj, :].bitcast(F32)
+            words = x_tiles[i][:].bitcast(F32)
             xt = psum.tile([P, PASSES, 2, P], F32, tag="xt", bufs=2)
             for g in range(PASSES):
                 for u in range(2):
@@ -126,38 +133,53 @@ def tile_multiheadlatentattention_pa_t_kernel(
 
         def quantise_x(i):
             x_grouped = live["x_grouped", i]
-            x_codes = work.tile([P, PASSES * P], U32, bufs=X_LEAD + 2, align_bytes=64)
-            x_scales = work.tile([P, PASSES * P], U8, bufs=X_LEAD + 2, align_bytes=64)
+            x_codes = work.tile([P, PASSES * P], U32, bufs=X_LEAD + ROPE_LAG + 1, align_bytes=64)
+            x_scales = work.tile([P, PASSES * P], U8, bufs=X_LEAD + ROPE_LAG + 1, align_bytes=64)
             nc.vector.quantize_mx(out=x_codes[:].bitcast(FP8X4), scales=x_scales[:], in_=x_grouped[:])
             live["x_mx", i] = (x_codes, x_scales)
 
-        def first_matmul(i):
+        def first_matmul(i, acc, n0):
             x_codes, x_scales = live["x_mx", i]
+            for g in range(PASSES):
+                tokens = slice(g * P, (g + 1) * P)
+                nc.tensor.matmul_mx(
+                    out=acc[:],
+                    lhsT=x_codes[:, tokens].bitcast(FP8X4),
+                    lhsT_scale=x_scales[:, tokens],
+                    rhs=w_codes[:, g, n0 : n0 + LORA].bitcast(FP8X4),
+                    rhs_scale=w_scales[:, g, n0 : n0 + LORA],
+                    start=(g == 0),
+                    stop=(g == PASSES - 1),
+                )
+
+        def matmul_lat(i):
             lat = psum.tile([P, LORA], F32, tag="lat", bufs=2)
-            kr = psum.tile([P, ROPE], F32, tag="kr", bufs=2)
-            for acc, n0 in ((lat, 0), (kr, LORA)):
-                for g in range(PASSES):
-                    tokens = slice(g * P, (g + 1) * P)
-                    nc.tensor.matmul_mx(
-                        out=acc[:],
-                        lhsT=x_codes[:, tokens].bitcast(FP8X4),
-                        lhsT_scale=x_scales[:, tokens],
-                        rhs=w_codes[:, g, n0 : n0 + LORA].bitcast(FP8X4),
-                        rhs_scale=w_scales[:, g, n0 : n0 + LORA],
-                        start=(g == 0),
-                        stop=(g == PASSES - 1),
-                    )
+            first_matmul(i, lat, 0)
             live["lat", i] = lat
+
+        def matmul_kr(i):
+            kr = psum.tile([P, ROPE], F32, tag="kr", bufs=2)
+            first_matmul(i, kr, LORA)
             live["kr", i] = kr
 
-        def mean_square(i):
+        def sum_squares(i):
             lat = live["lat", i]
             squares = work.tile([P, LORA], BF16)
             sum_sq = small.tile([P, 1], F32)
             nc.scalar.activation(out=squares[:], in_=lat[:], func=ACT.Square, accum_out=sum_sq[:])
+            live["sum_sq", i] = sum_sq
+
+        def root_mean_square(i):
             rms = small.tile([P, 1], F32)
-            nc.scalar.activation(out=rms[:], in_=sum_sq[:], func=ACT.Sqrt, bias=eps[:], scale=1.0 / LORA)
+            nc.scalar.activation(
+                out=rms[:], in_=live["sum_sq", i][:], func=ACT.Sqrt, bias=eps[:], scale=1.0 / LORA
+            )
             live["rms", i] = rms
+
+        def invert_rms(i):
+            inv_rms = small.tile([P, 1], F32)
+            nc.vector.reciprocal(out=inv_rms[:], in_=live["rms", i][:])
+            live["inv_rms", i] = inv_rms
 
         def rotate_products(i):
             kr = live["kr", i][:].rearrange("p (i e) -> p i e", e=2)
@@ -176,9 +198,7 @@ def tile_multiheadlatentattention_pa_t_kernel(
 
         def normalise(i):
             lat = live["lat", i]
-            rms = live["rms", i]
-            inv_rms = small.tile([P, 1], F32)
-            nc.vector.reciprocal(out=inv_rms[:], in_=rms[:])
+            inv_rms = live["inv_rms", i]
             n_bf16 = work.tile([P, LORA], BF16)
             nc.vector.scalar_tensor_tensor(
                 out=n_bf16[:], in0=lat[:], scalar=inv_rms[:], in1=gain[:], op0=ALU.mult, op1=ALU.mult
@@ -246,29 +266,36 @@ def tile_multiheadlatentattention_pa_t_kernel(
             nc.scalar.copy(out=kv_sb[:, i % OUT_TILES, :], in_=kv[:])
             store("kv_sb", kv_view, i)
 
-        for i in range(X_LEAD):
+        def regroup_piece(piece):
+            w_grouped = stage.tile([P, LORA, PACK], BF16, bufs=3, align_bytes=64)
+            regroup(nc, w_grouped, piece[0], LORA)
+            return w_grouped
+
+        def quantise_piece(piece, w_grouped):
+            nc.vector.quantize_mx(
+                out=piece[1].bitcast(FP8X4),
+                scales=piece[2],
+                in_=w_grouped[:].rearrange("p c t -> p (c t)"),
+            )
+
+        lat_pieces = [(lat_raws[g], w_codes[:, g, 0:LORA], w_scales[:, g, 0:LORA]) for g in range(PASSES)]
+        late_pieces = [
+            (rope_raws[g], w_codes[:, g, LORA : LORA + ROPE], w_scales[:, g, LORA : LORA + ROPE])
+            for g in range(PASSES)
+        ]
+        late_pieces.append((wd_raw, wd_codes[:], wd_scales[:]))
+
+        transpose_x(0)
+        group_x(0)
+        grouped_0 = regroup_piece(lat_pieces[0])
+        quantise_x(0)
+        grouped_1 = regroup_piece(lat_pieces[1])
+        quantise_piece(lat_pieces[0], grouped_0)
+        quantise_piece(lat_pieces[1], grouped_1)
+        for i in range(1, X_LEAD):
             transpose_x(i)
             group_x(i)
             quantise_x(i)
-
-        w_pieces = [
-            (w_raws[g][:, :, n0 : n0 + LORA], w_codes[:, g, n0 : n0 + LORA], w_scales[:, g, n0 : n0 + LORA])
-            for g in range(PASSES)
-            for n0 in (0, LORA)
-        ]
-        w_pieces.append((wd_raw[:], wd_codes[:], wd_scales[:]))
-        grouped_pieces = []
-        for k in range(len(w_pieces) + 1):
-            if k < len(w_pieces):
-                w_grouped = stage.tile([P, LORA, PACK], BF16, bufs=4, align_bytes=64)
-                regroup(nc, w_grouped, w_pieces[k][0], LORA)
-                grouped_pieces.append(w_grouped)
-            if k > 0:
-                nc.vector.quantize_mx(
-                    out=w_pieces[k - 1][1].bitcast(FP8X4),
-                    scales=w_pieces[k - 1][2],
-                    in_=grouped_pieces[k - 1][:].rearrange("p c t -> p (c t)"),
-                )
 
         gain_ps = psum.tile([P, LORA], F32, tag="kv")
         nc.tensor.matmul(gain_ps[:], lhsT=ones[:], rhs=gain_rows[:], start=True, stop=True)
@@ -278,17 +305,24 @@ def tile_multiheadlatentattention_pa_t_kernel(
             if 0 <= i < TILES:
                 stage_fn(i)
 
-        for s in range(TILES + 3):
+        for s in range(TILES + ROPE_LAG + 1):
             run(transpose_x, s + X_LEAD)
             run(transpose_n, s - 2)
             run(group_x, s + X_LEAD)
             run(group_n, s - 2)
-            run(first_matmul, s)
+            if s < len(late_pieces):
+                late_grouped = regroup_piece(late_pieces[s])
+            run(matmul_lat, s)
+            run(matmul_kr, s - ROPE_LAG)
             run(second_matmul, s - 3)
-            run(mean_square, s)
+            run(sum_squares, s)
             run(copy_kv, s - 3)
-            run(normalise, s - 1)
-            run(rotate_products, s - 1)
+            run(root_mean_square, s)
+            run(invert_rms, s - 1)
             run(quantise_x, s + X_LEAD)
+            run(normalise, s - 1)
+            run(rotate_products, s - ROPE_LAG - 1)
             run(quantise_n, s - 2)
-            run(rotate_sum, s - 1)
+            if s < len(late_pieces):
+                quantise_piece(late_pieces[s], late_grouped)
+            run(rotate_sum, s - ROPE_LAG - 1)

@@ -21,9 +21,9 @@ assert PASSES == 2
 J = T // P
 TILES = B * J
 HALF = ROPE // 2
-OUT_TILES = 2
 X_LEAD = 2
-ROPE_LAG = 2
+ROPE_LAG = 1
+LATE_PER_STEP = 2
 
 FLOPS = 2 * B * T * C * (LORA + ROPE) + 2 * B * T * LORA * KVW
 
@@ -52,7 +52,7 @@ def tile_multiheadlatentattention_pa_t_kernel(
         stage = ctx.enter_context(tc.tile_pool(name="stage", bufs=2))
         work = ctx.enter_context(tc.tile_pool(name="work", bufs=3))
         small = ctx.enter_context(tc.tile_pool(name="small", bufs=4))
-        outs = ctx.enter_context(tc.tile_pool(name="outs", bufs=3))
+        outs = ctx.enter_context(tc.tile_pool(name="outs", bufs=6))
         psum = ctx.enter_context(tc.psum_pool(name="psum", bufs=1))
         ctx.enter_context(tc.manual_schedule())
 
@@ -98,9 +98,9 @@ def tile_multiheadlatentattention_pa_t_kernel(
         load_x(2)
         rope_raws = load_w_half(LORA)
         load_x(1)
-        nc.sync.dma_start(out=table[:, 0 : J // 2, :], in_=table_view[:, 0 : J // 2, :])
         wd_raw = stage.tile([P, PACK, KVW], BF16, name="w_raw", bufs=2 * PASSES + 1)
         nc.sync.dma_start(out=wd_raw[:], in_=Wdkv.rearrange("(t p) n -> p t n", p=P))
+        nc.sync.dma_start(out=table[:, 0 : J // 2, :], in_=table_view[:, 0 : J // 2, :])
         load_x(2)
         nc.sync.dma_start(out=table[:, J // 2 : J, :], in_=table_view[:, J // 2 : J, :])
         load_x(TILES - len(x_tiles))
@@ -181,20 +181,28 @@ def tile_multiheadlatentattention_pa_t_kernel(
             nc.vector.reciprocal(out=inv_rms[:], in_=live["rms", i][:])
             live["inv_rms", i] = inv_rms
 
-        def rotate_products(i):
+        def pairs_of(i):
             kr = live["kr", i][:].rearrange("p (i e) -> p i e", e=2)
             cos_sin = table[:, i % J, :].rearrange("p (i two) -> p i two", two=2)
+            return kr, cos_sin
+
+        def rotate_by_cos(i):
+            kr, cos_sin = pairs_of(i)
             by_cos = work.tile([P, HALF, 2], F32)
             nc.vector.tensor_tensor(
                 out=by_cos[:], in0=kr, in1=cos_sin[:, :, 0:1].to_broadcast([P, HALF, 2]), op=ALU.mult
             )
+            live["by_cos", i] = by_cos
+
+        def rotate_by_sin(i):
+            kr, cos_sin = pairs_of(i)
             by_sin = work.tile([P, 2, HALF], F32)
             nc.vector.scalar_tensor_tensor(
                 out=by_sin[:, 0, :], in0=kr[:, :, 1], scalar=-1.0, in1=cos_sin[:, :, 1],
                 op0=ALU.mult, op1=ALU.mult,
             )
             nc.vector.tensor_tensor(out=by_sin[:, 1, :], in0=kr[:, :, 0], in1=cos_sin[:, :, 1], op=ALU.mult)
-            live["products", i] = (by_cos, by_sin)
+            live["by_sin", i] = by_sin
 
         def normalise(i):
             lat = live["lat", i]
@@ -205,26 +213,15 @@ def tile_multiheadlatentattention_pa_t_kernel(
             )
             live["n", i] = n_bf16
 
-        def out_slot(name, i):
-            if i % OUT_TILES == 0:
-                live[name] = outs.tile([P, OUT_TILES, KVW], F32, name=name)
-            return live[name]
-
-        def store(name, view, i):
-            if i % OUT_TILES == OUT_TILES - 1:
-                b, j = divmod(i, J)
-                nc.sync.dma_start(out=view[b, :, j + 1 - OUT_TILES : j + 1, :], in_=live[name][:])
-
         def rotate_sum(i):
-            by_cos, by_sin = live["products", i]
-            rope_sb = out_slot("rope_sb", i)
+            rope_sb = outs.tile([P, ROPE], F32)
             nc.gpsimd.tensor_tensor(
-                out=rope_sb[:, i % OUT_TILES, :].rearrange("p (i e) -> p i e", e=2),
-                in0=by_cos[:],
-                in1=by_sin[:].rearrange("p e i -> p i e"),
+                out=rope_sb[:].rearrange("p (i e) -> p i e", e=2),
+                in0=live["by_cos", i][:],
+                in1=live["by_sin", i][:].rearrange("p e i -> p i e"),
                 op=ALU.add,
             )
-            store("rope_sb", rope_view, i)
+            nc.sync.dma_start(out=rope_view[i // J, :, i % J, :], in_=rope_sb[:])
 
         def transpose_n(i):
             n_bf16 = live["n", i]
@@ -261,10 +258,9 @@ def tile_multiheadlatentattention_pa_t_kernel(
             live["kv", i] = kv
 
         def copy_kv(i):
-            kv = live["kv", i]
-            kv_sb = out_slot("kv_sb", i)
-            nc.scalar.copy(out=kv_sb[:, i % OUT_TILES, :], in_=kv[:])
-            store("kv_sb", kv_view, i)
+            kv_sb = outs.tile([P, KVW], F32)
+            nc.scalar.copy(out=kv_sb[:], in_=live["kv", i][:])
+            nc.sync.dma_start(out=kv_view[i // J, :, i % J, :], in_=kv_sb[:])
 
         def regroup_piece(piece):
             w_grouped = stage.tile([P, LORA, PACK], BF16, bufs=3, align_bytes=64)
@@ -305,13 +301,13 @@ def tile_multiheadlatentattention_pa_t_kernel(
             if 0 <= i < TILES:
                 stage_fn(i)
 
-        for s in range(TILES + ROPE_LAG + 1):
+        for s in range(TILES + 3):
+            late_now = late_pieces[LATE_PER_STEP * s : LATE_PER_STEP * (s + 1)]
             run(transpose_x, s + X_LEAD)
             run(transpose_n, s - 2)
             run(group_x, s + X_LEAD)
             run(group_n, s - 2)
-            if s < len(late_pieces):
-                late_grouped = regroup_piece(late_pieces[s])
+            late_grouped = [regroup_piece(piece) for piece in late_now]
             run(matmul_lat, s)
             run(matmul_kr, s - ROPE_LAG)
             run(second_matmul, s - 3)
@@ -319,10 +315,11 @@ def tile_multiheadlatentattention_pa_t_kernel(
             run(copy_kv, s - 3)
             run(root_mean_square, s)
             run(invert_rms, s - 1)
-            run(quantise_x, s + X_LEAD)
+            run(rotate_by_cos, s - ROPE_LAG - 1)
             run(normalise, s - 1)
-            run(rotate_products, s - ROPE_LAG - 1)
+            run(rotate_by_sin, s - ROPE_LAG - 1)
+            run(quantise_x, s + X_LEAD)
             run(quantise_n, s - 2)
-            if s < len(late_pieces):
-                quantise_piece(late_pieces[s], late_grouped)
+            for piece, w_grouped in zip(late_now, late_grouped):
+                quantise_piece(piece, w_grouped)
             run(rotate_sum, s - ROPE_LAG - 1)

@@ -29,7 +29,7 @@ FLOPS = 2 * B * T * C * (LORA + ROPE) + 2 * B * T * LORA * KVW
 
 
 def regroup(nc, grouped, raw, cols):
-    split = cols * 5 // 8
+    split = cols * 3 // 4
     for copy, lo, hi in ((nc.vector.tensor_copy, 0, split), (nc.scalar.copy, split, cols)):
         copy(
             out=grouped[:, lo:hi, :].rearrange("p (c i) t -> p c t i", i=4),
@@ -172,7 +172,7 @@ def tile_multiheadlatentattention_pa_t_kernel(
         def root_mean_square(i):
             rms = small.tile([P, 1], F32)
             nc.scalar.activation(
-                out=rms[:], in_=live["sum_sq", i][:], func=ACT.Sqrt, bias=eps[:], scale=1.0 / LORA
+                out=rms[:], in_=live["sum_sq", i][:], func=ACT.Sqrt, bias=EPS, scale=1.0 / LORA
             )
             live["rms", i] = rms
 

from contextlib import ExitStack

import concourse.mybir as mybir
from concourse.masks import make_identity

F32 = mybir.dt.float32
BF16 = mybir.dt.bfloat16
U32 = mybir.dt.uint32
U8 = mybir.dt.uint8
FP8X4 = mybir.dt.float8_e4m3fn_x4
ALU = mybir.AluOpType
ACT = mybir.ActivationFunctionType

B, T, C, LORA, ROPE, KVW = 4, 1024, 1024, 512, 512, 512
EPS = 1e-6
P = 128
PACK = 4
K_PASS = P * PACK
PASSES = C // K_PASS
assert PASSES == 2
J = T // P
TILES = B * J
HALF = ROPE // 2
X_LEAD = 2
ROPE_LAG = 1
LATE_PER_STEP = 2

FLOPS = 2 * B * T * C * (LORA + ROPE) + 2 * B * T * LORA * KVW


def regroup(nc, grouped, raw, cols):
    split = cols * 3 // 4
    for copy, lo, hi in ((nc.vector.tensor_copy, 0, split), (nc.scalar.copy, split, cols)):
        copy(
            out=grouped[:, lo:hi, :].rearrange("p (c i) t -> p c t i", i=4),
            in_=raw[:, :, lo:hi].rearrange("p t (c i) -> p c t i", i=4),
        )


def tile_multiheadlatentattention_pa_t_kernel(
    tc, x, freq_cis, Wckv, kv_norm_w, Wdkv, out_0, out_1
):
    nc = tc.nc
    x_view = x.rearrange("b (p j) c -> b p j c", j=J)
    table_view = freq_cis.rearrange("(p j) i two -> p j (i two)", j=J)
    kv_view = out_0.rearrange("b (p j) f -> b p j f", j=J)
    rope_view = out_1.rearrange("b (p j) f -> b p j f", j=J)

    with ExitStack() as ctx:
        keep = ctx.enter_context(tc.tile_pool(name="keep", bufs=1))
        x_pool = ctx.enter_context(tc.tile_pool(name="x_pool", bufs=TILES))
        stage = ctx.enter_context(tc.tile_pool(name="stage", bufs=2))
        work = ctx.enter_context(tc.tile_pool(name="work", bufs=3))
        small = ctx.enter_context(tc.tile_pool(name="small", bufs=4))
        outs = ctx.enter_context(tc.tile_pool(name="outs", bufs=6))
        psum = ctx.enter_context(tc.psum_pool(name="psum", bufs=1))
        ctx.enter_context(tc.manual_schedule())

        eps = keep.tile([P, 1], F32)
        nc.vector.memset(eps[:], EPS)
        warm = keep.tile([P, 1], F32)
        nc.scalar.activation(out=warm[:], in_=eps[:], func=ACT.Sqrt)
        ident_f32 = keep.tile([P, P], F32)
        make_identity(nc, ident_f32[:])
        ident_bf16 = keep.tile([P, P], BF16)
        make_identity(nc, ident_bf16[:])
        ones = keep.tile([P, P], BF16)
        nc.vector.memset(ones[:], 1.0)
        gain_rows = keep.tile([P, LORA], BF16)
        nc.vector.memset(gain_rows[:], 0.0)

        x_tiles = []

        def load_x(count):
            for i in range(len(x_tiles), len(x_tiles) + count):
                b, j = divmod(i, J)
                x_sb = x_pool.tile([P, C], BF16, name="x_sb")
                nc.sync.dma_start(out=x_sb[:], in_=x_view[b, :, j, :])
                x_tiles.append(x_sb)

        def load_w_half(n0):
            raws = []
            for g in range(PASSES):
                w_raw = stage.tile([P, PACK, LORA], BF16, name="w_raw", bufs=2 * PASSES + 1)
                for u in range(2):
                    k0 = K_PASS * g + 2 * P * u
                    nc.sync.dma_start(
                        out=w_raw[:, 2 * u : 2 * u + 2, :],
                        in_=Wckv[k0 : k0 + 2 * P, n0 : n0 + LORA].rearrange("(q e) c -> q e c", e=2),
                    )
                raws.append(w_raw)
            return raws

        table = keep.tile([P, J, ROPE], BF16)
        load_x(1)
        lat_raws = load_w_half(0)
        nc.sync.dma_start(out=gain_rows[0:1, :], in_=kv_norm_w.unsqueeze(0))
        load_x(2)
        rope_raws = load_w_half(LORA)
        load_x(1)
        wd_raw = stage.tile([P, PACK, KVW], BF16, name="w_raw", bufs=2 * PASSES + 1)
        nc.sync.dma_start(out=wd_raw[:], in_=Wdkv.rearrange("(t p) n -> p t n", p=P))
        nc.sync.dma_start(out=table[:, 0 : J // 2, :], in_=table_view[:, 0 : J // 2, :])
        load_x(2)
        nc.sync.dma_start(out=table[:, J // 2 : J, :], in_=table_view[:, J // 2 : J, :])
        load_x(TILES - len(x_tiles))

        w_codes = keep.tile([P, PASSES, LORA + ROPE], U32, align_bytes=64)
        w_scales = keep.tile([P, PASSES, LORA + ROPE], U8, align_bytes=64)
        wd_codes = keep.tile([P, KVW], U32, align_bytes=64)
        wd_scales = keep.tile([P, KVW], U8, align_bytes=64)
        gain = keep.tile([P, LORA], F32)

        live = {}

        def transpose_x(i):
            words = x_tiles[i][:].bitcast(F32)
            xt = psum.tile([P, PASSES, 2, P], F32, tag="xt", bufs=2)
            for g in range(PASSES):
                for u in range(2):
                    w0 = (2 * g + u) * P
                    nc.tensor.transpose(xt[:, g, u, :], words[:, w0 : w0 + P], ident_f32[:])
            live["xt", i] = xt

        def group_x(i):
            xt = live["xt", i]
            x_grouped = work.tile([P, PASSES * P * PACK], BF16, align_bytes=64)
            nc.scalar.copy(
                out=x_grouped[:].bitcast(F32).rearrange("p (g r u) -> p g r u", g=PASSES, u=2),
                in_=xt[:].rearrange("p g u r -> p g r u"),
            )
            live["x_grouped", i] = x_grouped

        def quantise_x(i):
            x_grouped = live["x_grouped", i]
            x_codes = work.tile([P, PASSES * P], U32, bufs=X_LEAD + ROPE_LAG + 1, align_bytes=64)
            x_scales = work.tile([P, PASSES * P], U8, bufs=X_LEAD + ROPE_LAG + 1, align_bytes=64)
            nc.vector.quantize_mx(out=x_codes[:].bitcast(FP8X4), scales=x_scales[:], in_=x_grouped[:])
            live["x_mx", i] = (x_codes, x_scales)

        def first_matmul(i, acc, n0):
            x_codes, x_scales = live["x_mx", i]
            for g in range(PASSES):
                tokens = slice(g * P, (g + 1) * P)
                nc.tensor.matmul_mx(
                    out=acc[:],
                    lhsT=x_codes[:, tokens].bitcast(FP8X4),
                    lhsT_scale=x_scales[:, tokens],
                    rhs=w_codes[:, g, n0 : n0 + LORA].bitcast(FP8X4),
                    rhs_scale=w_scales[:, g, n0 : n0 + LORA],
                    start=(g == 0),
                    stop=(g == PASSES - 1),
                )

        def matmul_lat(i):
            lat = psum.tile([P, LORA], F32, tag="lat", bufs=2)
            first_matmul(i, lat, 0)
            live["lat", i] = lat

        def matmul_kr(i):
            kr = psum.tile([P, ROPE], F32, tag="kr", bufs=2)
            first_matmul(i, kr, LORA)
            live["kr", i] = kr

        def sum_squares(i):
            lat = live["lat", i]
            squares = work.tile([P, LORA], BF16)
            sum_sq = small.tile([P, 1], F32)
            nc.scalar.activation(out=squares[:], in_=lat[:], func=ACT.Square, accum_out=sum_sq[:])
            live["sum_sq", i] = sum_sq

        def root_mean_square(i):
            rms = small.tile([P, 1], F32)
            nc.scalar.activation(
                out=rms[:], in_=live["sum_sq", i][:], func=ACT.Sqrt, bias=EPS, scale=1.0 / LORA
            )
            live["rms", i] = rms

        def invert_rms(i):
            inv_rms = small.tile([P, 1], F32)
            nc.vector.reciprocal(out=inv_rms[:], in_=live["rms", i][:])
            live["inv_rms", i] = inv_rms

        def pairs_of(i):
            kr = live["kr", i][:].rearrange("p (i e) -> p i e", e=2)
            cos_sin = table[:, i % J, :].rearrange("p (i two) -> p i two", two=2)
            return kr, cos_sin

        def rotate_by_cos(i):
            kr, cos_sin = pairs_of(i)
            by_cos = work.tile([P, HALF, 2], F32)
            nc.vector.tensor_tensor(
                out=by_cos[:], in0=kr, in1=cos_sin[:, :, 0:1].to_broadcast([P, HALF, 2]), op=ALU.mult
            )
            live["by_cos", i] = by_cos

        def rotate_by_sin(i):
            kr, cos_sin = pairs_of(i)
            by_sin = work.tile([P, 2, HALF], F32)
            nc.vector.scalar_tensor_tensor(
                out=by_sin[:, 0, :], in0=kr[:, :, 1], scalar=-1.0, in1=cos_sin[:, :, 1],
                op0=ALU.mult, op1=ALU.mult,
            )
            nc.vector.tensor_tensor(out=by_sin[:, 1, :], in0=kr[:, :, 0], in1=cos_sin[:, :, 1], op=ALU.mult)
            live["by_sin", i] = by_sin

        def normalise(i):
            lat = live["lat", i]
            inv_rms = live["inv_rms", i]
            n_bf16 = work.tile([P, LORA], BF16)
            nc.vector.scalar_tensor_tensor(
                out=n_bf16[:], in0=lat[:], scalar=inv_rms[:], in1=gain[:], op0=ALU.mult, op1=ALU.mult
            )
            live["n", i] = n_bf16

        def rotate_sum(i):
            rope_sb = outs.tile([P, ROPE], F32)
            nc.gpsimd.tensor_tensor(
                out=rope_sb[:].rearrange("p (i e) -> p i e", e=2),
                in0=live["by_cos", i][:],
                in1=live["by_sin", i][:].rearrange("p e i -> p i e"),
                op=ALU.add,
            )
            nc.sync.dma_start(out=rope_view[i // J, :, i % J, :], in_=rope_sb[:])

        def transpose_n(i):
            n_bf16 = live["n", i]
            nt = psum.tile([P, PACK, P], BF16, tag="nt")
            for t in range(PACK):
                nc.tensor.transpose(nt[:, t, :], n_bf16[:, t * P : (t + 1) * P], ident_bf16[:])
            live["nt", i] = nt

        def group_n(i):
            nt = live["nt", i]
            n_grouped = work.tile([P, P, PACK], BF16, align_bytes=64)
            nc.scalar.copy(out=n_grouped[:], in_=nt[:].rearrange("p t r -> p r t"))
            live["n_grouped", i] = n_grouped

        def quantise_n(i):
            n_grouped = live["n_grouped", i]
            n_codes = work.tile([P, P], U32, align_bytes=64)
            n_scales = work.tile([P, P], U8, align_bytes=64)
            nc.vector.quantize_mx(
                out=n_codes[:].bitcast(FP8X4), scales=n_scales[:],
                in_=n_grouped[:].rearrange("p r t -> p (r t)"),
            )
            live["n_mx", i] = (n_codes, n_scales)

        def second_matmul(i):
            n_codes, n_scales = live["n_mx", i]
            kv = psum.tile([P, KVW], F32, tag="kv")
            nc.tensor.matmul_mx(
                out=kv[:],
                lhsT=n_codes[:].bitcast(FP8X4), lhsT_scale=n_scales[:],
                rhs=wd_codes[:].bitcast(FP8X4), rhs_scale=wd_scales[:],
                start=True, stop=True,
            )
            live["kv", i] = kv

        def copy_kv(i):
            kv_sb = outs.tile([P, KVW], F32)
            nc.scalar.copy(out=kv_sb[:], in_=live["kv", i][:])
            nc.sync.dma_start(out=kv_view[i // J, :, i % J, :], in_=kv_sb[:])

        def regroup_piece(piece):
            w_grouped = stage.tile([P, LORA, PACK], BF16, bufs=3, align_bytes=64)
            regroup(nc, w_grouped, piece[0], LORA)
            return w_grouped

        def quantise_piece(piece, w_grouped):
            nc.vector.quantize_mx(
                out=piece[1].bitcast(FP8X4),
                scales=piece[2],
                in_=w_grouped[:].rearrange("p c t -> p (c t)"),
            )

        lat_pieces = [(lat_raws[g], w_codes[:, g, 0:LORA], w_scales[:, g, 0:LORA]) for g in range(PASSES)]
        late_pieces = [
            (rope_raws[g], w_codes[:, g, LORA : LORA + ROPE], w_scales[:, g, LORA : LORA + ROPE])
            for g in range(PASSES)
        ]
        late_pieces.append((wd_raw, wd_codes[:], wd_scales[:]))

        transpose_x(0)
        group_x(0)
        grouped_0 = regroup_piece(lat_pieces[0])
        quantise_x(0)
        grouped_1 = regroup_piece(lat_pieces[1])
        quantise_piece(lat_pieces[0], grouped_0)
        quantise_piece(lat_pieces[1], grouped_1)
        for i in range(1, X_LEAD):
            transpose_x(i)
            group_x(i)
            quantise_x(i)

        gain_ps = psum.tile([P, LORA], F32, tag="kv")
        nc.tensor.matmul(gain_ps[:], lhsT=ones[:], rhs=gain_rows[:], start=True, stop=True)
        nc.scalar.copy(out=gain[:], in_=gain_ps[:])

        def run(stage_fn, i):
            if 0 <= i < TILES:
                stage_fn(i)

        for s in range(TILES + 3):
            late_now = late_pieces[LATE_PER_STEP * s : LATE_PER_STEP * (s + 1)]
            run(transpose_x, s + X_LEAD)
            run(transpose_n, s - 2)
            run(group_x, s + X_LEAD)
            run(group_n, s - 2)
            late_grouped = [regroup_piece(piece) for piece in late_now]
            run(matmul_lat, s)
            run(matmul_kr, s - ROPE_LAG)
            run(second_matmul, s - 3)
            run(sum_squares, s)
            run(copy_kv, s - 3)
            run(root_mean_square, s)
            run(invert_rms, s - 1)
            run(rotate_by_cos, s - ROPE_LAG - 1)
            run(normalise, s - 1)
            run(rotate_by_sin, s - ROPE_LAG - 1)
            run(quantise_x, s + X_LEAD)
            run(quantise_n, s - 2)
            for piece, w_grouped in zip(late_now, late_grouped):
                quantise_piece(piece, w_grouped)
            run(rotate_sum, s - ROPE_LAG - 1)
